import numpy as np
import ml_dtypes


def mxq(x, axis, fmt="e4m3"):
    dtype, down = {"e4m3": (ml_dtypes.float8_e4m3fn, 7), "e5m2": (ml_dtypes.float8_e5m2, 14)}[fmt]
    v = np.moveaxis(np.asarray(x, np.float32).astype(ml_dtypes.bfloat16).astype(np.float64), axis, -1)
    blocks = v.reshape(v.shape[:-1] + (-1, 32))
    amax = np.abs(blocks).max(-1, keepdims=True)
    byte = np.maximum(np.where(amax > 0, np.frexp(amax)[1] - 1 + 127, 0) - down, 1)
    scale = np.exp2(byte - 127.0)
    codes = (blocks / scale).astype(np.float32).astype(dtype).astype(np.float64)
    return np.moveaxis((codes * scale).reshape(v.shape), -1, axis)


WIDE = False


def mx_kscale(k):
    if not WIDE:
        return np.ones(k)
    levels = np.array([10, -10, 5, -5, 0])
    if k % 512:
        return np.exp2(np.random.permutation(np.resize(levels, k // 32))).repeat(32)
    a = np.empty((k // 512, 16))
    for p in range(k // 512):
        a[p, :8] = np.random.permutation(np.resize(levels, 8))
        for g in range(8):
            far = levels[np.abs(levels - a[p, g]) >= 10]
            a[p, g + 8] = far[np.random.randint(len(far))]
    return np.exp2(a.ravel()).repeat(32)


BF16 = ml_dtypes.bfloat16


def bf(x):
    return np.asarray(x, np.float32).astype(BF16)


def f64(x):
    return np.asarray(x).astype(np.float64)


B, S, D, H, DN, DR, DV, RQ, RKV = 2, 256, 2048, 16, 64, 128, 128, 1536, 512
THETA = 10000.0
EPS = 1e-6


def rmsnorm(v, w):
    return v * (1.0 / np.sqrt(np.mean(v * v, axis=-1, keepdims=True) + EPS)) * w


def rotate_half(v):
    v1 = v[..., ::2]
    v2 = v[..., 1::2]
    return np.stack((-v2, v1), axis=-1).reshape(v.shape)


def rope_cache():
    inv_freq = 1.0 / THETA ** (np.arange(0, DR, 2) / DR)
    freqs = np.outer(np.arange(S), inv_freq)
    emb = np.concatenate((freqs, freqs), -1)
    return np.cos(emb), np.sin(emb)


def apply_rope(v, cos, sin):
    return v * cos[None, None] + rotate_half(v) * sin[None, None]


def setup_inputs():
    s, t = mx_kscale(D), mx_kscale(RQ)
    return {"x": bf(np.random.standard_normal((B, S, D)) * s),
            "Wqa": bf(np.random.standard_normal((D, RQ)) / np.sqrt(D) / s[:, None]),
            "q_a_norm_w": bf((1.0 + 0.1 * np.random.standard_normal(RQ)) * t),
            "Wqb": bf(np.random.standard_normal((RQ, H * (DN + DR))) / np.sqrt(RQ) / t[:, None])}


def reference(x, Wqa, q_a_norm_w, Wqb):
    c = mxq(f64(x), 2, "e4m3") @ mxq(f64(Wqa), 0, "e4m3")
    h = rmsnorm(c, f64(q_a_norm_w))
    q = mxq(h, 2, "e4m3") @ mxq(f64(Wqb), 0, "e4m3")
    q = q.reshape(B, S, H, DN + DR).transpose(0, 2, 1, 3)
    q_nope, q_rope = q[..., :DN], q[..., DN:]
    cos, sin = rope_cache()
    q_rope = apply_rope(q_rope, cos, sin)
    return np.concatenate([q_nope, q_rope], -1)

@@ -1,0 +1,449 @@
+from contextlib import ExitStack
+import math
+
+import concourse.mybir as mybir
+from concourse.masks import make_identity
+
+F32 = mybir.dt.float32
+BF16 = mybir.dt.bfloat16
+I32 = mybir.dt.int32
+U32 = mybir.dt.uint32
+U8 = mybir.dt.uint8
+FP8X4 = mybir.dt.float8_e4m3fn_x4
+ALU = mybir.AluOpType
+ACT = mybir.ActivationFunctionType
+
+P = 128
+PACK = 4
+K_PASS = P * PACK
+BANK = 512
+
+BATCH, SEQ, D_MODEL, HEADS, D_NOPE, D_ROPE, RANK = 2, 256, 2048, 16, 64, 128, 1536
+D_HEAD = D_NOPE + D_ROPE
+THETA = 10000.0
+EPS = 1e-6
+N_FREQ = D_ROPE // 2
+
+TOK_TILES = BATCH * SEQ // P
+SEQ_TILES = SEQ // P
+X_PASSES = D_MODEL // K_PASS
+H_PASSES = RANK // K_PASS
+RANK_BANKS = RANK // BANK
+GROUP_HEADS = 4
+GROUPS = HEADS // GROUP_HEADS
+GROUP_COLS = GROUP_HEADS * D_HEAD
+ROPE_COLS = GROUP_HEADS * D_ROPE
+NOPE_COLS = GROUP_HEADS * D_NOPE
+ROUND_MAGIC = 12582912.0
+
+FLOPS = 2 * BATCH * SEQ * (D_MODEL * RANK + RANK * HEADS * D_HEAD)
+
+
+def regroup(copy, grouped, rows):
+    copy(
+        out=grouped.rearrange("p (n c i) t -> p n c t i", n=rows.shape[2], i=4),
+        in_=rows.rearrange("p t n (c i) -> p n c t i", i=4),
+    )
+
+
+def build_rope_tables(nc, const):
+    position_int = const.tile([P, SEQ_TILES], I32)
+    nc.gpsimd.iota(position_int[:], pattern=[[P, SEQ_TILES]], base=0, channel_multiplier=1)
+    position = const.tile([P, SEQ_TILES], F32)
+    nc.vector.tensor_copy(out=position[:], in_=position_int[:])
+
+    freq = const.tile([P, N_FREQ], F32)
+    nc.vector.memset(freq[:, 0:1], 1.0)
+    for level in range(6):
+        span = 1 << level
+        nc.vector.tensor_scalar(
+            out=freq[:, span : 2 * span],
+            in0=freq[:, 0:span],
+            scalar1=THETA ** (-span / N_FREQ),
+            scalar2=None,
+            op0=ALU.mult,
+        )
+
+    turns = const.tile([P, 2, SEQ_TILES, N_FREQ], F32)
+    for a in range(SEQ_TILES):
+        nc.vector.tensor_scalar(
+            out=turns[:, 0, a, :],
+            in0=freq[:],
+            scalar1=position[:, a : a + 1],
+            scalar2=1.0 / (2.0 * math.pi),
+            op0=ALU.mult,
+            op1=ALU.mult,
+        )
+    nc.vector.tensor_scalar(
+        out=turns[:, 1], in0=turns[:, 0], scalar1=0.25, scalar2=None, op0=ALU.add
+    )
+    whole = const.tile([P, 2, SEQ_TILES, N_FREQ], F32)
+    nc.vector.tensor_scalar(
+        out=whole[:],
+        in0=turns[:],
+        scalar1=ROUND_MAGIC,
+        scalar2=ROUND_MAGIC,
+        op0=ALU.add,
+        op1=ALU.subtract,
+    )
+    part = const.tile([P, 2, SEQ_TILES, N_FREQ], F32)
+    nc.vector.tensor_tensor(out=part[:], in0=turns[:], in1=whole[:], op=ALU.subtract)
+    trig = const.tile([P, 2, SEQ_TILES, N_FREQ], F32)
+    nc.scalar.activation(out=trig[:], in_=part[:], func=ACT.Sin, scale=2.0 * math.pi)
+    warm = const.tile([P, 1], F32)
+    nc.scalar.sqrt(out=warm[:], in_=freq[:, 0:1])
+
+    sin_pairs = trig[:, 0].rearrange("p a (i e) -> p a i e", e=2)
+    neg_sin_even = const.tile([P, SEQ_TILES, N_FREQ // 2], F32)
+    nc.vector.tensor_scalar(
+        out=neg_sin_even[:], in0=sin_pairs[:, :, :, 0], scalar1=-1.0, scalar2=None, op0=ALU.mult
+    )
+    sin_odd = const.tile([P, SEQ_TILES, N_FREQ // 2], F32)
+    nc.vector.tensor_copy(out=sin_odd[:], in_=sin_pairs[:, :, :, 1])
+    return trig[:, 1], neg_sin_even, sin_odd
+
+
+def tile_multiheadlatentattention_pa_kernel(tc, x, Wqa, q_a_norm_w, Wqb, out):
+    nc = tc.nc
+    x_rows = x.flatten_outer_dims()
+
+    with ExitStack() as ctx:
+        const = ctx.enter_context(tc.tile_pool(name="const", bufs=1))
+        keep = ctx.enter_context(tc.tile_pool(name="keep", bufs=1))
+        grouped_pool = ctx.enter_context(tc.tile_pool(name="grouped", bufs=4))
+        norm_pool = ctx.enter_context(tc.tile_pool(name="norm", bufs=2))
+        psum = ctx.enter_context(tc.psum_pool(name="psum", bufs=8))
+
+        x_codes = keep.tile([P, TOK_TILES, X_PASSES * P], U32, align_bytes=64)
+        x_scales = keep.tile([P, TOK_TILES, X_PASSES * P], U8, align_bytes=64)
+        wqa_codes = keep.tile([P, X_PASSES, RANK], U32, align_bytes=64)
+        wqa_scales = keep.tile([P, X_PASSES, RANK], U8, align_bytes=64)
+        h_codes = keep.tile([P, TOK_TILES, H_PASSES, P], U32, align_bytes=64)
+        h_scales = keep.tile([P, TOK_TILES, H_PASSES, P], U8, align_bytes=64)
+        rope_codes = keep.tile([P, GROUPS, H_PASSES, ROPE_COLS], U32, align_bytes=64)
+        rope_scales = keep.tile([P, GROUPS, H_PASSES, ROPE_COLS], U8, align_bytes=64)
+        nope_codes = keep.tile([P, GROUPS, H_PASSES, NOPE_COLS], U32, align_bytes=64)
+        nope_scales = keep.tile([P, GROUPS, H_PASSES, NOPE_COLS], U8, align_bytes=64)
+
+        ident_f32 = const.tile([P, P], F32)
+        make_identity(nc, ident_f32[:])
+        ident_bf16 = const.tile([P, P], BF16)
+        make_identity(nc, ident_bf16[:])
+        cos_table, neg_sin_even, sin_odd = build_rope_tables(nc, const)
+
+        gain_row = const.tile([P, RANK], BF16)
+        nc.vector.memset(gain_row[:].bitcast(I32), 0)
+        nc.sync.dma_start(out=gain_row[0:1, :], in_=q_a_norm_w.unsqueeze(0))
+        ones = const.tile([P, P], BF16)
+        nc.vector.memset(ones[:], 1.0)
+        gain = const.tile([P, RANK], BF16)
+        for n in range(RANK_BANKS):
+            cols = slice(n * BANK, (n + 1) * BANK)
+            gain_bank = psum.tile([P, BANK], F32, tag="bank")
+            nc.tensor.matmul(
+                out=gain_bank[:], lhsT=ones[:], rhs=gain_row[:, cols], start=True, stop=True
+            )
+            nc.vector.tensor_copy(out=gain[:, cols], in_=gain_bank[:])
+
+        def quantise(grouped, codes, scales):
+            nc.vector.quantize_mx(
+                out=codes.bitcast(FP8X4), scales=scales, in_=grouped.rearrange("p c t -> p (c t)")
+            )
+
+        def new_c_banks(i):
+            return [
+                psum.tile([P, BANK], F32, tag="bank", name="c_%d_%d" % (i, n))
+                for n in range(RANK_BANKS)
+            ]
+
+        def first_matmul(c_banks, i, g, banks):
+            for n in banks:
+                nc.tensor.matmul_mx(
+                    out=c_banks[n][:],
+                    lhsT=x_codes[:, i, g * P : (g + 1) * P].bitcast(FP8X4),
+                    lhsT_scale=x_scales[:, i, g * P : (g + 1) * P],
+                    rhs=wqa_codes[:, g, n * BANK : (n + 1) * BANK].bitcast(FP8X4),
+                    rhs_scale=wqa_scales[:, g, n * BANK : (n + 1) * BANK],
+                    start=(g == 0),
+                    stop=(g == X_PASSES - 1),
+                )
+
+        c_banks = {}
+        with tc.tile_pool(name="x", bufs=TOK_TILES) as x_pool, tc.tile_pool(
+            name="wqa_raw", bufs=X_PASSES
+        ) as wqa_pool:
+            def load_x(i):
+                x_sb = x_pool.tile([P, D_MODEL], BF16)
+                nc.sync.dma_start(out=x_sb[:], in_=x_rows[i * P : (i + 1) * P, :])
+                return x_sb
+
+            x_tiles = [load_x(i) for i in range(2)]
+            wqa_tiles = []
+            for g in range(X_PASSES):
+                wqa_raw = wqa_pool.tile([P, PACK, RANK], BF16)
+                nc.sync.dma_start(
+                    out=wqa_raw[:],
+                    in_=Wqa[g * K_PASS : (g + 1) * K_PASS, :].rearrange(
+                        "(p t) c -> p t c", t=PACK
+                    ),
+                )
+                wqa_tiles.append(wqa_raw)
+            x_tiles.extend([load_x(i) for i in range(2, TOK_TILES)])
+
+            def quantise_x(i):
+                x_words = x_tiles[i][:].bitcast(F32)
+                x_grouped = x_pool.tile([P, D_MODEL], BF16, bufs=2, align_bytes=64)
+                x_grouped_words = x_grouped[:].bitcast(F32).rearrange(
+                    "p (g r u) -> p g r u", g=X_PASSES, u=2
+                )
+                for half in range(2):
+                    x_t = psum.tile([P, 2, 2, P], F32, tag="bank")
+                    for gg in range(2):
+                        for u in range(2):
+                            first = (2 * half + gg) * 2 * P
+                            nc.tensor.transpose(
+                                x_t[:, gg, u, :],
+                                x_words[:, first + u : first + 2 * P : 2],
+                                ident_f32[:],
+                            )
+                    nc.scalar.copy(
+                        out=x_grouped_words[:, 2 * half : 2 * half + 2],
+                        in_=x_t[:].rearrange("p g u r -> p g r u"),
+                    )
+                nc.vector.quantize_mx(
+                    out=x_codes[:, i, :].bitcast(FP8X4), scales=x_scales[:, i, :], in_=x_grouped[:]
+                )
+
+            for i in range(2):
+                quantise_x(i)
+
+            for i in range(2):
+                c_banks[i] = new_c_banks(i)
+            for g in range(X_PASSES):
+                blocks = []
+                for n in range(RANK_BANKS):
+                    on_vector = (g * RANK_BANKS + n) % 2 == 1
+                    wqa_grouped = grouped_pool.tile(
+                        [P, BANK, PACK], BF16, tag="grouped_512", align_bytes=64
+                    )
+                    regroup(
+                        nc.vector.tensor_copy if on_vector else nc.scalar.copy,
+                        wqa_grouped[:],
+                        wqa_tiles[g][:, :, n * BANK : (n + 1) * BANK].unsqueeze(2),
+                    )
+                    blocks.append(wqa_grouped)
+                for n in range(RANK_BANKS):
+                    cols = slice(n * BANK, (n + 1) * BANK)
+                    quantise(blocks[n][:], wqa_codes[:, g, cols], wqa_scales[:, g, cols])
+                for i in range(2):
+                    first_matmul(c_banks[i], i, g, range(RANK_BANKS))
+            for i in range(2, TOK_TILES):
+                quantise_x(i)
+
+        wqb_pool = ctx.enter_context(tc.tile_pool(name="wqb_raw", bufs=6, reuse_waits="tile"))
+        rope_pool = ctx.enter_context(tc.tile_pool(name="rope", bufs=3, reuse_waits="tile"))
+
+        wqb_tiles = {}
+        for r in range(GROUPS):
+            for g in range(H_PASSES):
+                wqb_raw = wqb_pool.tile([P, PACK, GROUP_COLS], BF16)
+                nc.sync.dma_start(
+                    out=wqb_raw[:],
+                    in_=Wqb[
+                        g * K_PASS : (g + 1) * K_PASS, r * GROUP_COLS : (r + 1) * GROUP_COLS
+                    ].rearrange("(p t) c -> p t c", t=PACK),
+                )
+                wqb_tiles[(r, g)] = wqb_raw
+
+        wqb_grouped = {}
+
+        def regroup_wqb(r, g):
+            by_head = wqb_tiles[(r, g)][:].rearrange("p t (h f) -> p t h f", f=D_HEAD)
+            rope_grouped = grouped_pool.tile(
+                [P, ROPE_COLS, PACK], BF16, tag="grouped_512", align_bytes=64
+            )
+            if r < 2:
+                regroup(nc.vector.tensor_copy, rope_grouped[:], by_head[:, :, :, D_NOPE:D_HEAD])
+            else:
+                for h in range(GROUP_HEADS):
+                    regroup(
+                        nc.scalar.copy,
+                        rope_grouped[:, h * D_ROPE : (h + 1) * D_ROPE, :],
+                        by_head[:, :, h : h + 1, D_NOPE:D_HEAD],
+                    )
+            nope_grouped = grouped_pool.tile(
+                [P, NOPE_COLS, PACK], BF16, tag="grouped_256", align_bytes=64
+            )
+            regroup(nc.scalar.copy, nope_grouped[:], by_head[:, :, :, 0:D_NOPE])
+            wqb_grouped[(r, g)] = (rope_grouped, nope_grouped)
+
+        def quantise_wqb(r, g):
+            rope_grouped, nope_grouped = wqb_grouped[(r, g)]
+            quantise(rope_grouped[:], rope_codes[:, r, g, :], rope_scales[:, r, g, :])
+            quantise(nope_grouped[:], nope_codes[:, r, g, :], nope_scales[:, r, g, :])
+
+        sum_sq = {}
+        rstd = {}
+        h_rows = {}
+        h_grouped = {}
+
+        def square(i, n):
+            if n == 0:
+                sum_sq[i] = norm_pool.tile([P, RANK_BANKS], F32, name="sum_sq")
+            squares = norm_pool.tile([P, BANK], BF16)
+            nc.scalar.activation(
+                out=squares[:],
+                in_=c_banks[i][n][:],
+                func=ACT.Square,
+                accum_out=sum_sq[i][:, n : n + 1],
+            )
+
+        def mean_square(i):
+            rstd[i] = norm_pool.tile([P, 1], F32, name="rstd")
+            nc.vector.tensor_reduce(
+                out=rstd[i][:], in_=sum_sq[i][:], axis=mybir.AxisListType.X, op=ALU.add
+            )
+            nc.vector.tensor_scalar(
+                out=rstd[i][:],
+                in0=rstd[i][:],
+                scalar1=1.0 / RANK,
+                scalar2=EPS,
+                op0=ALU.mult,
+                op1=ALU.add,
+            )
+
+        def scale_and_transpose(i, n):
+            if n == 0:
+                h_rows[i] = norm_pool.tile([P, RANK], BF16, name="h_rows")
+            cols = slice(n * BANK, (n + 1) * BANK)
+            nc.vector.scalar_tensor_tensor(
+                out=h_rows[i][:, cols],
+                in0=c_banks[i][n][:],
+                scalar=rstd[i][:, 0:1],
+                in1=gain[:, cols],
+                op0=ALU.mult,
+                op1=ALU.mult,
+            )
+            h_t = psum.tile([P, PACK, P], BF16, tag="bank")
+            for t in range(PACK):
+                columns = slice(n * K_PASS + t, (n + 1) * K_PASS, PACK)
+                nc.tensor.transpose(h_t[:, t, :], h_rows[i][:, columns], ident_bf16[:])
+            h_grouped[(i, n)] = h_t
+
+        def copy_h(i, g):
+            h_t = h_grouped[(i, g)]
+            h_words = norm_pool.tile([P, P, PACK], BF16, bufs=6, align_bytes=64)
+            nc.scalar.copy(out=h_words[:], in_=h_t[:].rearrange("p t r -> p r t"))
+            h_grouped[(i, g)] = h_words
+
+        def quantise_h(i, g):
+            quantise(h_grouped[(i, g)][:], h_codes[:, i, g, :], h_scales[:, i, g, :])
+
+        def norm_front(i):
+            for n in range(RANK_BANKS):
+                square(i, n)
+
+        def move_c_to_sbuf(i):
+            c_rows = norm_pool.tile([P, RANK], F32)
+            for n in range(RANK_BANKS):
+                nc.vector.tensor_copy(out=c_rows[:, n * BANK : (n + 1) * BANK], in_=c_banks[i][n][:])
+            c_banks[i] = [c_rows[:, n * BANK : (n + 1) * BANK] for n in range(RANK_BANKS)]
+
+        def norm_middle(i):
+            mean_square(i)
+            nc.scalar.sqrt(out=rstd[i][:], in_=rstd[i][:])
+            nc.vector.reciprocal(out=rstd[i][:], in_=rstd[i][:])
+            for n in range(RANK_BANKS):
+                scale_and_transpose(i, n)
+
+        def norm_back(i):
+            for g in range(H_PASSES):
+                copy_h(i, g)
+            for g in range(H_PASSES):
+                quantise_h(i, g)
+
+        for i in range(2):
+            norm_front(i)
+            move_c_to_sbuf(i)
+        for i in range(2, TOK_TILES):
+            c_banks[i] = new_c_banks(i)
+            for n in range(RANK_BANKS):
+                for g in range(X_PASSES):
+                    first_matmul(c_banks[i], i, g, [n])
+        for i in range(2):
+            norm_middle(i)
+        for i in range(2):
+            norm_back(i)
+        for i in range(2, TOK_TILES):
+            norm_front(i)
+        for i in range(2, TOK_TILES):
+            norm_middle(i)
+        for i in range(2, TOK_TILES):
+            norm_back(i)
+        for g in range(H_PASSES):
+            regroup_wqb(0, g)
+        for g in range(H_PASSES):
+            quantise_wqb(0, g)
+
+        def second_matmul_and_rope(r, i):
+            rope_q = psum.tile([P, ROPE_COLS], F32, tag="bank")
+            nope_q = psum.tile([P, NOPE_COLS], F32, tag="bank")
+            for g in range(H_PASSES):
+                for q_bank, codes, scales in (
+                    (rope_q, rope_codes, rope_scales),
+                    (nope_q, nope_codes, nope_scales),
+                ):
+                    nc.tensor.matmul_mx(
+                        out=q_bank[:],
+                        lhsT=h_codes[:, i, g, :].bitcast(FP8X4),
+                        lhsT_scale=h_scales[:, i, g, :],
+                        rhs=codes[:, r, g, :].bitcast(FP8X4),
+                        rhs_scale=scales[:, r, g, :],
+                        start=(g == 0),
+                        stop=(g == H_PASSES - 1),
+                    )
+
+            a = i % SEQ_TILES
+            result = rope_pool.tile([P, GROUP_HEADS, D_HEAD], F32, bufs=6)
+            nc.scalar.copy(
+                out=result[:, :, 0:D_NOPE], in_=nope_q[:].rearrange("p (h f) -> p h f", f=D_NOPE)
+            )
+            repeats = ROPE_COLS // N_FREQ
+            straight = rope_pool.tile([P, ROPE_COLS], F32, bufs=5)
+            nc.vector.tensor_tensor(
+                out=straight[:].rearrange("p (m j) -> p m j", j=N_FREQ),
+                in0=rope_q[:].rearrange("p (m j) -> p m j", j=N_FREQ),
+                in1=cos_table[:, a, :].unsqueeze(1).to_broadcast([P, repeats, N_FREQ]),
+                op=ALU.mult,
+            )
+            crossed = rope_pool.tile([P, 2, ROPE_COLS // 2], F32, bufs=5)
+            pairs = rope_q[:].rearrange("p (m i e) -> p m i e", i=N_FREQ // 2, e=2)
+            for e, table in ((0, neg_sin_even), (1, sin_odd)):
+                nc.vector.tensor_tensor(
+                    out=crossed[:, e, :].rearrange("p (m i) -> p m i", i=N_FREQ // 2),
+                    in0=pairs[:, :, :, 1 - e],
+                    in1=table[:, a, :].unsqueeze(1).to_broadcast([P, repeats, N_FREQ // 2]),
+                    op=ALU.mult,
+                )
+            last = r == GROUPS - 1 and i == TOK_TILES - 1
+            adder = nc.vector if last else nc.gpsimd
+            adder.tensor_tensor(
+                out=result[:, :, D_NOPE:D_HEAD].rearrange("p h (i e) -> p h i e", e=2),
+                in0=straight[:].rearrange("p (h i e) -> p h i e", h=GROUP_HEADS, e=2),
+                in1=crossed[:].rearrange("p e (h i) -> p h i e", h=GROUP_HEADS),
+                op=ALU.add,
+            )
+            nc.sync.dma_start(
+                out=out[
+                    i // SEQ_TILES, r * GROUP_HEADS : (r + 1) * GROUP_HEADS, a * P : (a + 1) * P, :
+                ].rearrange("h s f -> s h f"),
+                in_=result[:],
+            )
+
+        for r in range(GROUPS):
+            for i in range(TOK_TILES):
+                if r + 1 < GROUPS and i < H_PASSES:
+                    regroup_wqb(r + 1, i)
+                second_matmul_and_rope(r, i)
+                if r + 1 < GROUPS and i > 0:
+                    quantise_wqb(r + 1, i - 1)

@@ -90,17 +90,15 @@ def build_rope_tables(nc, const):
     nc.vector.tensor_tensor(out=part[:], in0=turns[:], in1=whole[:], op=ALU.subtract)
     trig = const.tile([P, 2, SEQ_TILES, N_FREQ], F32)
     nc.scalar.activation(out=trig[:], in_=part[:], func=ACT.Sin, scale=2.0 * math.pi)
-    warm = const.tile([P, 1], F32)
-    nc.scalar.sqrt(out=warm[:], in_=freq[:, 0:1])
-
     sin_pairs = trig[:, 0].rearrange("p a (i e) -> p a i e", e=2)
-    neg_sin_even = const.tile([P, SEQ_TILES, N_FREQ // 2], F32)
     nc.vector.tensor_scalar(
-        out=neg_sin_even[:], in0=sin_pairs[:, :, :, 0], scalar1=-1.0, scalar2=None, op0=ALU.mult
+        out=sin_pairs[:, :, :, 0],
+        in0=sin_pairs[:, :, :, 0],
+        scalar1=-1.0,
+        scalar2=None,
+        op0=ALU.mult,
     )
-    sin_odd = const.tile([P, SEQ_TILES, N_FREQ // 2], F32)
-    nc.vector.tensor_copy(out=sin_odd[:], in_=sin_pairs[:, :, :, 1])
-    return trig[:, 1], neg_sin_even, sin_odd
+    return trig[:, 1], trig[:, 0]
 
 
 def tile_multiheadlatentattention_pa_kernel(tc, x, Wqa, q_a_norm_w, Wqb, out):
@@ -127,9 +125,7 @@ def tile_multiheadlatentattention_pa_kernel(tc, x, Wqa, q_a_norm_w, Wqb, out):
 
         ident_f32 = const.tile([P, P], F32)
         make_identity(nc, ident_f32[:])
-        ident_bf16 = const.tile([P, P], BF16)
-        make_identity(nc, ident_bf16[:])
-        cos_table, neg_sin_even, sin_odd = build_rope_tables(nc, const)
+        cos_table, sin_table = build_rope_tables(nc, const)
 
         gain_row = const.tile([P, RANK], BF16)
         nc.vector.memset(gain_row[:].bitcast(I32), 0)
@@ -137,18 +133,23 @@ def tile_multiheadlatentattention_pa_kernel(tc, x, Wqa, q_a_norm_w, Wqb, out):
         ones = const.tile([P, P], BF16)
         nc.vector.memset(ones[:], 1.0)
         gain = const.tile([P, RANK], BF16)
-        for n in range(RANK_BANKS):
-            cols = slice(n * BANK, (n + 1) * BANK)
-            gain_bank = psum.tile([P, BANK], F32, tag="bank")
-            nc.tensor.matmul(
-                out=gain_bank[:], lhsT=ones[:], rhs=gain_row[:, cols], start=True, stop=True
-            )
-            nc.vector.tensor_copy(out=gain[:, cols], in_=gain_bank[:])
+
+        def spread_gain():
+            for n in range(RANK_BANKS):
+                cols = slice(n * BANK, (n + 1) * BANK)
+                gain_bank = psum.tile([P, BANK], BF16, tag="bank")
+                nc.tensor.matmul(
+                    out=gain_bank[:], lhsT=ones[:], rhs=gain_row[:, cols], start=True, stop=True
+                )
+                nc.vector.tensor_copy(out=gain[:, cols], in_=gain_bank[:])
 
         def quantise(grouped, codes, scales):
             nc.vector.quantize_mx(
                 out=codes.bitcast(FP8X4), scales=scales, in_=grouped.rearrange("p c t -> p (c t)")
             )
+
+        minus_half = const.tile([P, 1], F32)
+        nc.gpsimd.memset(minus_half[:], -0.5)
 
         def new_c_banks(i):
             return [
@@ -170,24 +171,33 @@ def tile_multiheadlatentattention_pa_kernel(tc, x, Wqa, q_a_norm_w, Wqb, out):
 
         c_banks = {}
         with tc.tile_pool(name="x", bufs=TOK_TILES) as x_pool, tc.tile_pool(
-            name="wqa_raw", bufs=X_PASSES
+            name="wqa_raw", bufs=3
         ) as wqa_pool:
             def load_x(i):
                 x_sb = x_pool.tile([P, D_MODEL], BF16)
                 nc.sync.dma_start(out=x_sb[:], in_=x_rows[i * P : (i + 1) * P, :])
                 return x_sb
 
-            x_tiles = [load_x(i) for i in range(2)]
-            wqa_tiles = []
-            for g in range(X_PASSES):
-                wqa_raw = wqa_pool.tile([P, PACK, RANK], BF16)
+            wqa_blocks = {}
+
+            def load_wqa(g, first, blocks):
+                wqa_raw = wqa_pool.tile(
+                    [P, PACK, blocks * BANK], BF16, name="wqa_raw_%d" % blocks
+                )
                 nc.sync.dma_start(
                     out=wqa_raw[:],
-                    in_=Wqa[g * K_PASS : (g + 1) * K_PASS, :].rearrange(
-                        "(p t) c -> p t c", t=PACK
-                    ),
+                    in_=Wqa[
+                        g * K_PASS : (g + 1) * K_PASS, first * BANK : (first + blocks) * BANK
+                    ].rearrange("(p t) c -> p t c", t=PACK),
                 )
-                wqa_tiles.append(wqa_raw)
+                for n in range(blocks):
+                    wqa_blocks[(g, first + n)] = wqa_raw[:, :, n * BANK : (n + 1) * BANK]
+
+            for n in range(RANK_BANKS):
+                load_wqa(0, n, 1)
+            x_tiles = [load_x(i) for i in range(2)]
+            for g in range(1, X_PASSES):
+                load_wqa(g, 0, RANK_BANKS)
             x_tiles.extend([load_x(i) for i in range(2, TOK_TILES)])
 
             def quantise_x(i):
@@ -222,14 +232,14 @@ def tile_multiheadlatentattention_pa_kernel(tc, x, Wqa, q_a_norm_w, Wqb, out):
             for g in range(X_PASSES):
                 blocks = []
                 for n in range(RANK_BANKS):
-                    on_vector = (g * RANK_BANKS + n) % 2 == 1
+                    on_vector = (g * RANK_BANKS + n) % 2 == 0
                     wqa_grouped = grouped_pool.tile(
                         [P, BANK, PACK], BF16, tag="grouped_512", align_bytes=64
                     )
                     regroup(
                         nc.vector.tensor_copy if on_vector else nc.scalar.copy,
                         wqa_grouped[:],
-                        wqa_tiles[g][:, :, n * BANK : (n + 1) * BANK].unsqueeze(2),
+                        wqa_blocks[(g, n)].unsqueeze(2),
                     )
                     blocks.append(wqa_grouped)
                 for n in range(RANK_BANKS):
@@ -237,6 +247,7 @@ def tile_multiheadlatentattention_pa_kernel(tc, x, Wqa, q_a_norm_w, Wqb, out):
                     quantise(blocks[n][:], wqa_codes[:, g, cols], wqa_scales[:, g, cols])
                 for i in range(2):
                     first_matmul(c_banks[i], i, g, range(RANK_BANKS))
+            spread_gain()
             for i in range(2, TOK_TILES):
                 quantise_x(i)
 
@@ -324,16 +335,24 @@ def tile_multiheadlatentattention_pa_kernel(tc, x, Wqa, q_a_norm_w, Wqb, out):
                 op0=ALU.mult,
                 op1=ALU.mult,
             )
-            h_t = psum.tile([P, PACK, P], BF16, tag="bank")
-            for t in range(PACK):
-                columns = slice(n * K_PASS + t, (n + 1) * K_PASS, PACK)
-                nc.tensor.transpose(h_t[:, t, :], h_rows[i][:, columns], ident_bf16[:])
+            h_t = psum.tile([P, 2, P], F32, tag="bank")
+            h_pairs = h_rows[i][:].bitcast(F32)
+            for u in range(2):
+                first = n * 2 * P + u
+                nc.tensor.transpose(
+                    h_t[:, u, :], h_pairs[:, first : (n + 1) * 2 * P : 2], ident_f32[:]
+                )
             h_grouped[(i, n)] = h_t
 
         def copy_h(i, g):
             h_t = h_grouped[(i, g)]
             h_words = norm_pool.tile([P, P, PACK], BF16, bufs=6, align_bytes=64)
-            nc.scalar.copy(out=h_words[:], in_=h_t[:].rearrange("p t r -> p r t"))
+            nc.scalar.copy(
+                out=h_words[:].rearrange("p r t -> p (r t)").bitcast(F32).rearrange(
+                    "p (r u) -> p r u", u=2
+                ),
+                in_=h_t[:].rearrange("p u r -> p r u"),
+            )
             h_grouped[(i, g)] = h_words
 
         def quantise_h(i, g):
@@ -343,16 +362,11 @@ def tile_multiheadlatentattention_pa_kernel(tc, x, Wqa, q_a_norm_w, Wqb, out):
             for n in range(RANK_BANKS):
                 square(i, n)
 
-        def move_c_to_sbuf(i):
-            c_rows = norm_pool.tile([P, RANK], F32)
-            for n in range(RANK_BANKS):
-                nc.vector.tensor_copy(out=c_rows[:, n * BANK : (n + 1) * BANK], in_=c_banks[i][n][:])
-            c_banks[i] = [c_rows[:, n * BANK : (n + 1) * BANK] for n in range(RANK_BANKS)]
-
         def norm_middle(i):
             mean_square(i)
-            nc.scalar.sqrt(out=rstd[i][:], in_=rstd[i][:])
-            nc.vector.reciprocal(out=rstd[i][:], in_=rstd[i][:])
+            nc.gpsimd.tensor_tensor(
+                out=rstd[i][:], in0=rstd[i][:], in1=minus_half[:], op=ALU.pow
+            )
             for n in range(RANK_BANKS):
                 scale_and_transpose(i, n)
 
@@ -364,21 +378,17 @@ def tile_multiheadlatentattention_pa_kernel(tc, x, Wqa, q_a_norm_w, Wqb, out):
 
         for i in range(2):
             norm_front(i)
-            move_c_to_sbuf(i)
+        for i in range(2):
+            norm_middle(i)
         for i in range(2, TOK_TILES):
             c_banks[i] = new_c_banks(i)
             for n in range(RANK_BANKS):
                 for g in range(X_PASSES):
                     first_matmul(c_banks[i], i, g, [n])
-        for i in range(2):
-            norm_middle(i)
-        for i in range(2):
-            norm_back(i)
-        for i in range(2, TOK_TILES):
             norm_front(i)
+            norm_back(i - 2)
         for i in range(2, TOK_TILES):
             norm_middle(i)
-        for i in range(2, TOK_TILES):
             norm_back(i)
         for g in range(H_PASSES):
             regroup_wqb(0, g)
@@ -416,21 +426,22 @@ def tile_multiheadlatentattention_pa_kernel(tc, x, Wqa, q_a_norm_w, Wqb, out):
                 in1=cos_table[:, a, :].unsqueeze(1).to_broadcast([P, repeats, N_FREQ]),
                 op=ALU.mult,
             )
-            crossed = rope_pool.tile([P, 2, ROPE_COLS // 2], F32, bufs=5)
-            pairs = rope_q[:].rearrange("p (m i e) -> p m i e", i=N_FREQ // 2, e=2)
-            for e, table in ((0, neg_sin_even), (1, sin_odd)):
-                nc.vector.tensor_tensor(
-                    out=crossed[:, e, :].rearrange("p (m i) -> p m i", i=N_FREQ // 2),
-                    in0=pairs[:, :, :, 1 - e],
-                    in1=table[:, a, :].unsqueeze(1).to_broadcast([P, repeats, N_FREQ // 2]),
-                    op=ALU.mult,
-                )
+            crossed = rope_pool.tile([P, ROPE_COLS], F32, bufs=5)
+            nc.vector.tensor_tensor(
+                out=crossed[:].rearrange("p (m i e) -> p m i e", i=N_FREQ // 2, e=2),
+                in0=rope_q[:].rearrange("p (m i e) -> p m i e", i=N_FREQ // 2, e=2)[:, :, :, ::-1],
+                in1=sin_table[:, a, :]
+                .rearrange("p (i e) -> p i e", e=2)
+                .unsqueeze(1)
+                .to_broadcast([P, repeats, N_FREQ // 2, 2]),
+                op=ALU.mult,
+            )
             last = r == GROUPS - 1 and i == TOK_TILES - 1
             adder = nc.vector if last else nc.gpsimd
             adder.tensor_tensor(
-                out=result[:, :, D_NOPE:D_HEAD].rearrange("p h (i e) -> p h i e", e=2),
-                in0=straight[:].rearrange("p (h i e) -> p h i e", h=GROUP_HEADS, e=2),
-                in1=crossed[:].rearrange("p e (h i) -> p h i e", h=GROUP_HEADS),
+                out=result[:, :, D_NOPE:D_HEAD],
+                in0=straight[:].rearrange("p (h f) -> p h f", h=GROUP_HEADS),
+                in1=crossed[:].rearrange("p (h f) -> p h f", h=GROUP_HEADS),
                 op=ALU.add,
             )
             nc.sync.dma_start(

@@ -36,6 +36,8 @@ ROPE_COLS = GROUP_HEADS * D_ROPE
 NOPE_COLS = GROUP_HEADS * D_NOPE
 ROUND_MAGIC = 12582912.0
 
+BLOCKS = X_PASSES * RANK_BANKS
+
 FLOPS = 2 * BATCH * SEQ * (D_MODEL * RANK + RANK * HEADS * D_HEAD)
 
 
@@ -91,7 +93,7 @@ def build_rope_tables(nc, const):
     trig = const.tile([P, 2, SEQ_TILES, N_FREQ], F32)
     nc.scalar.activation(out=trig[:], in_=part[:], func=ACT.Sin, scale=2.0 * math.pi)
     sin_pairs = trig[:, 0].rearrange("p a (i e) -> p a i e", e=2)
-    nc.vector.tensor_scalar(
+    nc.gpsimd.tensor_scalar(
         out=sin_pairs[:, :, :, 0],
         in0=sin_pairs[:, :, :, 0],
         scalar1=-1.0,
@@ -108,6 +110,7 @@ def tile_multiheadlatentattention_pa_kernel(tc, x, Wqa, q_a_norm_w, Wqb, out):
     with ExitStack() as ctx:
         const = ctx.enter_context(tc.tile_pool(name="const", bufs=1))
         keep = ctx.enter_context(tc.tile_pool(name="keep", bufs=1))
+        late_x_pool = ctx.enter_context(tc.tile_pool(name="late_x", bufs=2))
         grouped_pool = ctx.enter_context(tc.tile_pool(name="grouped", bufs=4))
         norm_pool = ctx.enter_context(tc.tile_pool(name="norm", bufs=2))
         psum = ctx.enter_context(tc.psum_pool(name="psum", bufs=8))
@@ -125,14 +128,11 @@ def tile_multiheadlatentattention_pa_kernel(tc, x, Wqa, q_a_norm_w, Wqb, out):
 
         ident_f32 = const.tile([P, P], F32)
         make_identity(nc, ident_f32[:])
-        cos_table, sin_table = build_rope_tables(nc, const)
-
         gain_row = const.tile([P, RANK], BF16)
-        nc.vector.memset(gain_row[:].bitcast(I32), 0)
-        nc.sync.dma_start(out=gain_row[0:1, :], in_=q_a_norm_w.unsqueeze(0))
+        nc.gpsimd.memset(gain_row[:].bitcast(I32), 0)
         ones = const.tile([P, P], BF16)
-        nc.vector.memset(ones[:], 1.0)
         gain = const.tile([P, RANK], BF16)
+        minus_half = const.tile([P, 1], F32)
 
         def spread_gain():
             for n in range(RANK_BANKS):
@@ -141,15 +141,12 @@ def tile_multiheadlatentattention_pa_kernel(tc, x, Wqa, q_a_norm_w, Wqb, out):
                 nc.tensor.matmul(
                     out=gain_bank[:], lhsT=ones[:], rhs=gain_row[:, cols], start=True, stop=True
                 )
-                nc.vector.tensor_copy(out=gain[:, cols], in_=gain_bank[:])
+                nc.scalar.copy(out=gain[:, cols], in_=gain_bank[:])
 
         def quantise(grouped, codes, scales):
             nc.vector.quantize_mx(
                 out=codes.bitcast(FP8X4), scales=scales, in_=grouped.rearrange("p c t -> p (c t)")
             )
-
-        minus_half = const.tile([P, 1], F32)
-        nc.gpsimd.memset(minus_half[:], -0.5)
 
         def new_c_banks(i):
             return [
@@ -157,32 +154,59 @@ def tile_multiheadlatentattention_pa_kernel(tc, x, Wqa, q_a_norm_w, Wqb, out):
                 for n in range(RANK_BANKS)
             ]
 
-        def first_matmul(c_banks, i, g, banks):
-            for n in banks:
-                nc.tensor.matmul_mx(
-                    out=c_banks[n][:],
-                    lhsT=x_codes[:, i, g * P : (g + 1) * P].bitcast(FP8X4),
-                    lhsT_scale=x_scales[:, i, g * P : (g + 1) * P],
-                    rhs=wqa_codes[:, g, n * BANK : (n + 1) * BANK].bitcast(FP8X4),
-                    rhs_scale=wqa_scales[:, g, n * BANK : (n + 1) * BANK],
-                    start=(g == 0),
-                    stop=(g == X_PASSES - 1),
+        c_banks = {}
+
+        def first_matmul(i, g, n):
+            nc.tensor.matmul_mx(
+                out=c_banks[i][n][:],
+                lhsT=x_codes[:, i, g * P : (g + 1) * P].bitcast(FP8X4),
+                lhsT_scale=x_scales[:, i, g * P : (g + 1) * P],
+                rhs=wqa_codes[:, g, n * BANK : (n + 1) * BANK].bitcast(FP8X4),
+                rhs_scale=wqa_scales[:, g, n * BANK : (n + 1) * BANK],
+                start=(g == 0),
+                stop=(g == X_PASSES - 1),
+            )
+
+        x_tiles = {}
+        x_grouped = {}
+
+        def load_x(i, pool):
+            x_sb = pool.tile([P, D_MODEL], BF16, name="x_sb")
+            nc.sync.dma_start(out=x_sb[:], in_=x_rows[i * P : (i + 1) * P, :])
+            x_tiles[i] = x_sb
+
+        def transpose_x(i):
+            x_words = x_tiles[i][:].bitcast(F32)
+            x_grouped[i] = late_x_pool.tile([P, D_MODEL], BF16, name="x_grouped", align_bytes=64)
+            x_grouped_words = x_grouped[i][:].bitcast(F32).rearrange(
+                "p (g r u) -> p g r u", g=X_PASSES, u=2
+            )
+            for half in range(2):
+                x_t = psum.tile([P, 2, 2, P], F32, tag="bank")
+                for gg in range(2):
+                    for u in range(2):
+                        first = (2 * half + gg) * 2 * P
+                        nc.tensor.transpose(
+                            x_t[:, gg, u, :],
+                            x_words[:, first + u : first + 2 * P : 2],
+                            ident_f32[:],
+                        )
+                nc.scalar.copy(
+                    out=x_grouped_words[:, 2 * half : 2 * half + 2],
+                    in_=x_t[:].rearrange("p g u r -> p g r u"),
                 )
 
-        c_banks = {}
-        with tc.tile_pool(name="x", bufs=TOK_TILES) as x_pool, tc.tile_pool(
-            name="wqa_raw", bufs=3
-        ) as wqa_pool:
-            def load_x(i):
-                x_sb = x_pool.tile([P, D_MODEL], BF16)
-                nc.sync.dma_start(out=x_sb[:], in_=x_rows[i * P : (i + 1) * P, :])
-                return x_sb
+        def quantise_x(i):
+            nc.vector.quantize_mx(
+                out=x_codes[:, i, :].bitcast(FP8X4), scales=x_scales[:, i, :], in_=x_grouped[i][:]
+            )
 
+        with tc.tile_pool(name="x", bufs=2) as x_pool, tc.tile_pool(name="wqa_raw", bufs=1) as wqa_pool:
             wqa_blocks = {}
 
             def load_wqa(g, first, blocks):
                 wqa_raw = wqa_pool.tile(
-                    [P, PACK, blocks * BANK], BF16, name="wqa_raw_%d" % blocks
+                    [P, PACK, blocks * BANK], BF16, name="wqa_raw_%d_%d" % (g, first)
                 )
                 nc.sync.dma_start(
                     out=wqa_raw[:],
@@ -193,123 +217,130 @@ def tile_multiheadlatentattention_pa_kernel(tc, x, Wqa, q_a_norm_w, Wqb, out):
                 for n in range(blocks):
                     wqa_blocks[(g, first + n)] = wqa_raw[:, :, n * BANK : (n + 1) * BANK]
 
-            for n in range(RANK_BANKS):
-                load_wqa(0, n, 1)
-            x_tiles = [load_x(i) for i in range(2)]
-            for g in range(1, X_PASSES):
-                load_wqa(g, 0, RANK_BANKS)
-            x_tiles.extend([load_x(i) for i in range(2, TOK_TILES)])
+            load_wqa(0,0,1)
+            load_wqa(0,1,1)
+            load_wqa(0,2,1)
+            load_wqa(1,0,1)
+            load_wqa(1,1,2)
+            load_x(0, x_pool)
+            load_x(1, x_pool)
+            nc.sync.dma_start(out=gain_row[0:1, :], in_=q_a_norm_w.unsqueeze(0))
+            load_wqa(2,0,3)
+            load_wqa(3,0,1)
+            load_wqa(3,1,2)
 
-            def quantise_x(i):
-                x_words = x_tiles[i][:].bitcast(F32)
-                x_grouped = x_pool.tile([P, D_MODEL], BF16, bufs=2, align_bytes=64)
-                x_grouped_words = x_grouped[:].bitcast(F32).rearrange(
-                    "p (g r u) -> p g r u", g=X_PASSES, u=2
+            nc.gpsimd.memset(ones[:], 1.0)
+            nc.gpsimd.memset(minus_half[:], -0.5)
+
+            grouped = {}
+
+            def regroup_wqa(b):
+                g, n = divmod(b, RANK_BANKS)
+                grouped[b] = grouped_pool.tile(
+                    [P, BANK, PACK], BF16, name="wqa_grouped", tag="grouped_512", align_bytes=64
                 )
-                for half in range(2):
-                    x_t = psum.tile([P, 2, 2, P], F32, tag="bank")
-                    for gg in range(2):
-                        for u in range(2):
-                            first = (2 * half + gg) * 2 * P
-                            nc.tensor.transpose(
-                                x_t[:, gg, u, :],
-                                x_words[:, first + u : first + 2 * P : 2],
-                                ident_f32[:],
-                            )
-                    nc.scalar.copy(
-                        out=x_grouped_words[:, 2 * half : 2 * half + 2],
-                        in_=x_t[:].rearrange("p g u r -> p g r u"),
-                    )
-                nc.vector.quantize_mx(
-                    out=x_codes[:, i, :].bitcast(FP8X4), scales=x_scales[:, i, :], in_=x_grouped[:]
+                regroup(
+                    nc.vector.tensor_copy if b % 2 == 0 else nc.scalar.copy,
+                    grouped[b][:],
+                    wqa_blocks[(g, n)].unsqueeze(2),
                 )
 
-            for i in range(2):
-                quantise_x(i)
+            def quantise_wqa(b):
+                g, n = divmod(b, RANK_BANKS)
+                cols = slice(n * BANK, (n + 1) * BANK)
+                quantise(grouped[b][:], wqa_codes[:, g, cols], wqa_scales[:, g, cols])
 
             for i in range(2):
                 c_banks[i] = new_c_banks(i)
-            for g in range(X_PASSES):
-                blocks = []
+            for b in range(BLOCKS + 2):
+                if b < BLOCKS:
+                    regroup_wqa(b)
+                if b in (5, 6):
+                    transpose_x(b - 5)
+                if b in (7, 8):
+                    quantise_x(b - 7)
+                if b >= 2:
+                    quantise_wqa(b - 2)
+                if b >= 9:
+                    g = b - 9
+                    if g < X_PASSES - 1:
+                        for i in range(2):
+                            for n in range(RANK_BANKS):
+                                first_matmul(i, g, n)
+            for i in range(2):
                 for n in range(RANK_BANKS):
-                    on_vector = (g * RANK_BANKS + n) % 2 == 0
-                    wqa_grouped = grouped_pool.tile(
-                        [P, BANK, PACK], BF16, tag="grouped_512", align_bytes=64
-                    )
-                    regroup(
-                        nc.vector.tensor_copy if on_vector else nc.scalar.copy,
-                        wqa_grouped[:],
-                        wqa_blocks[(g, n)].unsqueeze(2),
-                    )
-                    blocks.append(wqa_grouped)
-                for n in range(RANK_BANKS):
-                    cols = slice(n * BANK, (n + 1) * BANK)
-                    quantise(blocks[n][:], wqa_codes[:, g, cols], wqa_scales[:, g, cols])
-                for i in range(2):
-                    first_matmul(c_banks[i], i, g, range(RANK_BANKS))
-            spread_gain()
-            for i in range(2, TOK_TILES):
-                quantise_x(i)
+                    first_matmul(i, X_PASSES - 1, n)
 
-        wqb_pool = ctx.enter_context(tc.tile_pool(name="wqb_raw", bufs=6, reuse_waits="tile"))
-        rope_pool = ctx.enter_context(tc.tile_pool(name="rope", bufs=3, reuse_waits="tile"))
+        cos_table, sin_table = build_rope_tables(nc, const)
+
+        wqb_pool = ctx.enter_context(tc.tile_pool(name="wqb_raw", bufs=7, reuse_waits="tile"))
+        rope_pool = ctx.enter_context(tc.tile_pool(name="rope", bufs=4, reuse_waits="tile"))
 
         wqb_tiles = {}
-        for r in range(GROUPS):
-            for g in range(H_PASSES):
-                wqb_raw = wqb_pool.tile([P, PACK, GROUP_COLS], BF16)
-                nc.sync.dma_start(
-                    out=wqb_raw[:],
-                    in_=Wqb[
-                        g * K_PASS : (g + 1) * K_PASS, r * GROUP_COLS : (r + 1) * GROUP_COLS
-                    ].rearrange("(p t) c -> p t c", t=PACK),
+
+        def load_wqb(unit):
+            r, g = divmod(unit, H_PASSES)
+            wqb_raw = wqb_pool.tile([P, PACK, GROUP_COLS], BF16, name="wqb_raw")
+            nc.sync.dma_start(
+                out=wqb_raw[:],
+                in_=Wqb[
+                    g * K_PASS : (g + 1) * K_PASS, r * GROUP_COLS : (r + 1) * GROUP_COLS
+                ].rearrange("(p t) c -> p t c", t=PACK),
+            )
+            wqb_tiles[unit] = wqb_raw[:].rearrange("p t (h f) -> p t h f", f=D_HEAD)
+
+        for unit in range(7):
+            load_wqb(unit)
+            if unit < 2:
+                load_x(unit + 2, late_x_pool)
+
+        rope_grouped = {}
+        nope_grouped = {}
+
+        def regroup_rope(unit, copy, halves=(0, 1)):
+            if 0 in halves:
+                rope_grouped[unit] = grouped_pool.tile(
+                    [P, ROPE_COLS, PACK], BF16, name="rope_grouped", tag="grouped_512", align_bytes=64
                 )
-                wqb_tiles[(r, g)] = wqb_raw
+            for half in halves:
+                regroup(
+                    copy,
+                    rope_grouped[unit][:, half * 2 * D_ROPE : (half + 1) * 2 * D_ROPE, :],
+                    wqb_tiles[unit][:, :, 2 * half : 2 * half + 2, D_NOPE:D_HEAD],
+                )
 
-        wqb_grouped = {}
-
-        def regroup_wqb(r, g):
-            by_head = wqb_tiles[(r, g)][:].rearrange("p t (h f) -> p t h f", f=D_HEAD)
-            rope_grouped = grouped_pool.tile(
-                [P, ROPE_COLS, PACK], BF16, tag="grouped_512", align_bytes=64
+        def regroup_nope(unit, copy):
+            nope_grouped[unit] = grouped_pool.tile(
+                [P, NOPE_COLS, PACK], BF16, name="nope_grouped", tag="grouped_256", align_bytes=64
             )
-            if r < 2:
-                regroup(nc.vector.tensor_copy, rope_grouped[:], by_head[:, :, :, D_NOPE:D_HEAD])
-            else:
-                for h in range(GROUP_HEADS):
-                    regroup(
-                        nc.scalar.copy,
-                        rope_grouped[:, h * D_ROPE : (h + 1) * D_ROPE, :],
-                        by_head[:, :, h : h + 1, D_NOPE:D_HEAD],
-                    )
-            nope_grouped = grouped_pool.tile(
-                [P, NOPE_COLS, PACK], BF16, tag="grouped_256", align_bytes=64
-            )
-            regroup(nc.scalar.copy, nope_grouped[:], by_head[:, :, :, 0:D_NOPE])
-            wqb_grouped[(r, g)] = (rope_grouped, nope_grouped)
+            regroup(copy, nope_grouped[unit][:], wqb_tiles[unit][:, :, :, 0:D_NOPE])
 
-        def quantise_wqb(r, g):
-            rope_grouped, nope_grouped = wqb_grouped[(r, g)]
-            quantise(rope_grouped[:], rope_codes[:, r, g, :], rope_scales[:, r, g, :])
-            quantise(nope_grouped[:], nope_codes[:, r, g, :], nope_scales[:, r, g, :])
+        def quantise_rope(unit):
+            r, g = divmod(unit, H_PASSES)
+            quantise(rope_grouped[unit][:], rope_codes[:, r, g, :], rope_scales[:, r, g, :])
+
+        def quantise_nope(unit):
+            r, g = divmod(unit, H_PASSES)
+            quantise(nope_grouped[unit][:], nope_codes[:, r, g, :], nope_scales[:, r, g, :])
 
         sum_sq = {}
         rstd = {}
         h_rows = {}
-        h_grouped = {}
+        h_banks = {}
+        h_words = {}
 
-        def square(i, n):
-            if n == 0:
-                sum_sq[i] = norm_pool.tile([P, RANK_BANKS], F32, name="sum_sq")
-            squares = norm_pool.tile([P, BANK], BF16)
-            nc.scalar.activation(
-                out=squares[:],
-                in_=c_banks[i][n][:],
-                func=ACT.Square,
-                accum_out=sum_sq[i][:, n : n + 1],
-            )
+        def square(i):
+            sum_sq[i] = norm_pool.tile([P, RANK_BANKS], F32, name="sum_sq")
+            for n in range(RANK_BANKS):
+                squares = norm_pool.tile([P, BANK], BF16)
+                nc.scalar.activation(
+                    out=squares[:],
+                    in_=c_banks[i][n][:],
+                    func=ACT.Square,
+                    accum_out=sum_sq[i][:, n : n + 1],
+                )
 
-        def mean_square(i):
+        def inverse_rms(i):
             rstd[i] = norm_pool.tile([P, 1], F32, name="rstd")
             nc.vector.tensor_reduce(
                 out=rstd[i][:], in_=sum_sq[i][:], axis=mybir.AxisListType.X, op=ALU.add
@@ -322,87 +353,65 @@ def tile_multiheadlatentattention_pa_kernel(tc, x, Wqa, q_a_norm_w, Wqb, out):
                 op0=ALU.mult,
                 op1=ALU.add,
             )
+            nc.gpsimd.tensor_tensor(out=rstd[i][:], in0=rstd[i][:], in1=minus_half[:], op=ALU.pow)
 
-        def scale_and_transpose(i, n):
-            if n == 0:
-                h_rows[i] = norm_pool.tile([P, RANK], BF16, name="h_rows")
-            cols = slice(n * BANK, (n + 1) * BANK)
-            nc.vector.scalar_tensor_tensor(
-                out=h_rows[i][:, cols],
-                in0=c_banks[i][n][:],
-                scalar=rstd[i][:, 0:1],
-                in1=gain[:, cols],
-                op0=ALU.mult,
-                op1=ALU.mult,
-            )
-            h_t = psum.tile([P, 2, P], F32, tag="bank")
-            h_pairs = h_rows[i][:].bitcast(F32)
-            for u in range(2):
-                first = n * 2 * P + u
-                nc.tensor.transpose(
-                    h_t[:, u, :], h_pairs[:, first : (n + 1) * 2 * P : 2], ident_f32[:]
+        def scale_h(i):
+            h_rows[i] = norm_pool.tile([P, RANK], BF16, name="h_rows")
+            for n in range(RANK_BANKS):
+                cols = slice(n * BANK, (n + 1) * BANK)
+                nc.vector.scalar_tensor_tensor(
+                    out=h_rows[i][:, cols],
+                    in0=c_banks[i][n][:],
+                    scalar=rstd[i][:, 0:1],
+                    in1=gain[:, cols],
+                    op0=ALU.mult,
+                    op1=ALU.mult,
                 )
-            h_grouped[(i, n)] = h_t
 
-        def copy_h(i, g):
-            h_t = h_grouped[(i, g)]
-            h_words = norm_pool.tile([P, P, PACK], BF16, bufs=6, align_bytes=64)
-            nc.scalar.copy(
-                out=h_words[:].rearrange("p r t -> p (r t)").bitcast(F32).rearrange(
-                    "p (r u) -> p r u", u=2
-                ),
-                in_=h_t[:].rearrange("p u r -> p r u"),
-            )
-            h_grouped[(i, g)] = h_words
+        def transpose_h(i):
+            h_pairs = h_rows[i][:].bitcast(F32)
+            for n in range(H_PASSES):
+                h_t = psum.tile([P, 2, P], F32, tag="bank")
+                for u in range(2):
+                    first = n * 2 * P + u
+                    nc.tensor.transpose(
+                        h_t[:, u, :], h_pairs[:, first : (n + 1) * 2 * P : 2], ident_f32[:]
+                    )
+                h_banks[(i, n)] = h_t
 
-        def quantise_h(i, g):
-            quantise(h_grouped[(i, g)][:], h_codes[:, i, g, :], h_scales[:, i, g, :])
+        def copy_h(i):
+            for n in range(H_PASSES):
+                words = norm_pool.tile([P, P, PACK], BF16, bufs=6, align_bytes=64)
+                nc.scalar.copy(
+                    out=words[:].rearrange("p r t -> p (r t)").bitcast(F32).rearrange(
+                        "p (r u) -> p r u", u=2
+                    ),
+                    in_=h_banks[(i, n)][:].rearrange("p u r -> p r u"),
+                )
+                h_words[(i, n)] = words
 
-        def norm_front(i):
-            for n in range(RANK_BANKS):
-                square(i, n)
+        def quantise_h(i):
+            for n in range(H_PASSES):
+                quantise(h_words[(i, n)][:], h_codes[:, i, n, :], h_scales[:, i, n, :])
 
-        def norm_middle(i):
-            mean_square(i)
-            nc.gpsimd.tensor_tensor(
-                out=rstd[i][:], in0=rstd[i][:], in1=minus_half[:], op=ALU.pow
-            )
-            for n in range(RANK_BANKS):
-                scale_and_transpose(i, n)
-
-        def norm_back(i):
-            for g in range(H_PASSES):
-                copy_h(i, g)
-            for g in range(H_PASSES):
-                quantise_h(i, g)
-
-        for i in range(2):
-            norm_front(i)
-        for i in range(2):
-            norm_middle(i)
-        for i in range(2, TOK_TILES):
+        def multiply_again(i):
             c_banks[i] = new_c_banks(i)
             for n in range(RANK_BANKS):
                 for g in range(X_PASSES):
-                    first_matmul(c_banks[i], i, g, [n])
-            norm_front(i)
-            norm_back(i - 2)
-        for i in range(2, TOK_TILES):
-            norm_middle(i)
-            norm_back(i)
-        for g in range(H_PASSES):
-            regroup_wqb(0, g)
-        for g in range(H_PASSES):
-            quantise_wqb(0, g)
+                    first_matmul(i, g, n)
 
-        def second_matmul_and_rope(r, i):
-            rope_q = psum.tile([P, ROPE_COLS], F32, tag="bank")
-            nope_q = psum.tile([P, NOPE_COLS], F32, tag="bank")
-            for g in range(H_PASSES):
-                for q_bank, codes, scales in (
-                    (rope_q, rope_codes, rope_scales),
-                    (nope_q, nope_codes, nope_scales),
-                ):
+        rope_q = {}
+        nope_q = {}
+        results = {}
+
+        def second_matmul(r, i):
+            rope_q[(r, i)] = psum.tile([P, ROPE_COLS], F32, tag="bank", name="rope_q")
+            nope_q[(r, i)] = psum.tile([P, NOPE_COLS], F32, tag="bank", name="nope_q")
+            for q_bank, codes, scales in (
+                (rope_q[(r, i)], rope_codes, rope_scales),
+                (nope_q[(r, i)], nope_codes, nope_scales),
+            ):
+                for g in range(H_PASSES):
                     nc.tensor.matmul_mx(
                         out=q_bank[:],
                         lhsT=h_codes[:, i, g, :].bitcast(FP8X4),
@@ -413,33 +422,37 @@ def tile_multiheadlatentattention_pa_kernel(tc, x, Wqa, q_a_norm_w, Wqb, out):
                         stop=(g == H_PASSES - 1),
                     )
 
-            a = i % SEQ_TILES
-            result = rope_pool.tile([P, GROUP_HEADS, D_HEAD], F32, bufs=6)
+        def copy_nope(r, i):
+            results[(r, i)] = rope_pool.tile([P, GROUP_HEADS, D_HEAD], F32, name="result", bufs=6)
             nc.scalar.copy(
-                out=result[:, :, 0:D_NOPE], in_=nope_q[:].rearrange("p (h f) -> p h f", f=D_NOPE)
+                out=results[(r, i)][:, :, 0:D_NOPE],
+                in_=nope_q[(r, i)][:].rearrange("p (h f) -> p h f", f=D_NOPE),
             )
-            repeats = ROPE_COLS // N_FREQ
-            straight = rope_pool.tile([P, ROPE_COLS], F32, bufs=5)
+
+        repeats = ROPE_COLS // N_FREQ
+
+        def rotate(r, i, adder):
+            a = i % SEQ_TILES
+            bank = rope_q[(r, i)]
+            straight = rope_pool.tile([P, ROPE_COLS], F32)
             nc.vector.tensor_tensor(
                 out=straight[:].rearrange("p (m j) -> p m j", j=N_FREQ),
-                in0=rope_q[:].rearrange("p (m j) -> p m j", j=N_FREQ),
+                in0=bank[:].rearrange("p (m j) -> p m j", j=N_FREQ),
                 in1=cos_table[:, a, :].unsqueeze(1).to_broadcast([P, repeats, N_FREQ]),
                 op=ALU.mult,
             )
-            crossed = rope_pool.tile([P, ROPE_COLS], F32, bufs=5)
+            crossed = rope_pool.tile([P, ROPE_COLS], F32)
             nc.vector.tensor_tensor(
                 out=crossed[:].rearrange("p (m i e) -> p m i e", i=N_FREQ // 2, e=2),
-                in0=rope_q[:].rearrange("p (m i e) -> p m i e", i=N_FREQ // 2, e=2)[:, :, :, ::-1],
+                in0=bank[:].rearrange("p (m i e) -> p m i e", i=N_FREQ // 2, e=2)[:, :, :, ::-1],
                 in1=sin_table[:, a, :]
                 .rearrange("p (i e) -> p i e", e=2)
                 .unsqueeze(1)
                 .to_broadcast([P, repeats, N_FREQ // 2, 2]),
                 op=ALU.mult,
             )
-            last = r == GROUPS - 1 and i == TOK_TILES - 1
-            adder = nc.vector if last else nc.gpsimd
             adder.tensor_tensor(
-                out=result[:, :, D_NOPE:D_HEAD],
+                out=results[(r, i)][:, :, D_NOPE:D_HEAD],
                 in0=straight[:].rearrange("p (h f) -> p h f", h=GROUP_HEADS),
                 in1=crossed[:].rearrange("p (h f) -> p h f", h=GROUP_HEADS),
                 op=ALU.add,
@@ -448,13 +461,75 @@ def tile_multiheadlatentattention_pa_kernel(tc, x, Wqa, q_a_norm_w, Wqb, out):
                 out=out[
                     i // SEQ_TILES, r * GROUP_HEADS : (r + 1) * GROUP_HEADS, a * P : (a + 1) * P, :
                 ].rearrange("h s f -> s h f"),
-                in_=result[:],
+                in_=results[(r, i)][:],
             )
 
-        for r in range(GROUPS):
-            for i in range(TOK_TILES):
-                if r + 1 < GROUPS and i < H_PASSES:
-                    regroup_wqb(r + 1, i)
-                second_matmul_and_rope(r, i)
-                if r + 1 < GROUPS and i > 0:
-                    quantise_wqb(r + 1, i - 1)
+        vector_copy = nc.vector.tensor_copy
+        scalar_copy = nc.scalar.copy
+
+        transpose_x(2)
+        quantise_x(2)
+        spread_gain()
+        square(0)
+        regroup_nope(0, vector_copy)
+        transpose_x(3)
+        square(1)
+        inverse_rms(0)
+        quantise_x(3)
+        scale_h(0)
+        transpose_h(0)
+        regroup_rope(0, scalar_copy)
+        quantise_nope(0)
+        inverse_rms(1)
+        multiply_again(2)
+        scale_h(1)
+        transpose_h(1)
+        copy_h(0)
+        regroup_nope(1, vector_copy)
+        regroup_rope(1, scalar_copy)
+        quantise_h(0)
+        quantise_rope(0)
+        copy_h(1)
+        square(2)
+        multiply_again(3)
+        regroup_nope(2, vector_copy)
+        quantise_nope(1)
+        quantise_h(1)
+        inverse_rms(2)
+        quantise_rope(1)
+        regroup_rope(2, vector_copy)
+        scale_h(2)
+        transpose_h(2)
+        square(3)
+        quantise_nope(2)
+        quantise_rope(2)
+        copy_h(2)
+        inverse_rms(3)
+        second_matmul(0, 0)
+        quantise_h(2)
+        scale_h(3)
+        transpose_h(3)
+        regroup_rope(3, scalar_copy)
+        regroup_nope(3, vector_copy)
+        copy_h(3)
+        second_matmul(0, 1)
+        quantise_h(3)
+        quantise_rope(3)
+        quantise_nope(3)
+        for unit in range(7, H_PASSES * GROUPS):
+            load_wqb(unit)
+
+        steps = [(r, i) for r in range(GROUPS) for i in range(TOK_TILES)]
+        for s in range(len(steps)):
+            r, i = steps[s]
+            unit = H_PASSES * r + 4 + i
+            if i < H_PASSES and unit < H_PASSES * GROUPS:
+                regroup_rope(unit, scalar_copy)
+                regroup_nope(unit, vector_copy if unit < 9 else scalar_copy)
+            copy_nope(r, i)
+            rotate(r, i, nc.vector if s >= len(steps) - 2 else nc.gpsimd)
+            if i > 0 and unit - 1 < H_PASSES * GROUPS:
+                quantise_rope(unit - 1)
+                quantise_nope(unit - 1)
+            if s + 2 < len(steps):
+                second_matmul(*steps[s + 2])

@@ -36,6 +36,8 @@ ROPE_COLS = GROUP_HEADS * D_ROPE
 NOPE_COLS = GROUP_HEADS * D_NOPE
 ROUND_MAGIC = 12582912.0
 
+RUN = 8
+
 BLOCKS = X_PASSES * RANK_BANKS
 
 FLOPS = 2 * BATCH * SEQ * (D_MODEL * RANK + RANK * HEADS * D_HEAD)
@@ -43,8 +45,8 @@ FLOPS = 2 * BATCH * SEQ * (D_MODEL * RANK + RANK * HEADS * D_HEAD)
 
 def regroup(copy, grouped, rows):
     copy(
-        out=grouped.rearrange("p (n c i) t -> p n c t i", n=rows.shape[2], i=4),
-        in_=rows.rearrange("p t n (c i) -> p n c t i", i=4),
+        out=grouped.rearrange("p (n c i) t -> p n c t i", n=rows.shape[2], i=RUN),
+        in_=rows.rearrange("p t n (c i) -> p n c t i", i=RUN),
     )
 
 

@@ -242,7 +242,7 @@ def tile_multiheadlatentattention_pa_kernel(tc, x, Wqa, q_a_norm_w, Wqb, out):
                     [P, BANK, PACK], BF16, name="wqa_grouped", tag="grouped_512", align_bytes=64
                 )
                 regroup(
-                    nc.vector.tensor_copy if b % 2 == 0 else nc.scalar.copy,
+                    nc.vector.tensor_copy if b % 2 == 0 or b == BLOCKS - 1 else nc.scalar.copy,
                     grouped[b][:],
                     wqa_blocks[(g, n)].unsqueeze(2),
                 )
@@ -330,6 +330,7 @@ def tile_multiheadlatentattention_pa_kernel(tc, x, Wqa, q_a_norm_w, Wqb, out):
         h_rows = {}
         h_banks = {}
         h_words = {}
+        H_BANKS = ((0, 1), (2,))
 
         def square(i):
             sum_sq[i] = norm_pool.tile([P, RANK_BANKS], F32, name="sum_sq")
@@ -344,16 +345,15 @@ def tile_multiheadlatentattention_pa_kernel(tc, x, Wqa, q_a_norm_w, Wqb, out):
 
         def inverse_rms(i):
             rstd[i] = norm_pool.tile([P, 1], F32, name="rstd")
-            nc.vector.tensor_reduce(
-                out=rstd[i][:], in_=sum_sq[i][:], axis=mybir.AxisListType.X, op=ALU.add
-            )
+            shares = norm_pool.tile([P, RANK_BANKS], F32)
             nc.vector.tensor_scalar(
-                out=rstd[i][:],
-                in0=rstd[i][:],
+                out=shares[:],
+                in0=sum_sq[i][:],
                 scalar1=1.0 / RANK,
                 scalar2=EPS,
                 op0=ALU.mult,
                 op1=ALU.add,
+                accum_out=rstd[i][:],
             )
             nc.gpsimd.tensor_tensor(out=rstd[i][:], in0=rstd[i][:], in1=minus_half[:], op=ALU.pow)
 
@@ -372,29 +372,39 @@ def tile_multiheadlatentattention_pa_kernel(tc, x, Wqa, q_a_norm_w, Wqb, out):
 
         def transpose_h(i):
             h_pairs = h_rows[i][:].bitcast(F32)
-            for n in range(H_PASSES):
-                h_t = psum.tile([P, 2, P], F32, tag="bank")
-                for u in range(2):
-                    first = n * 2 * P + u
-                    nc.tensor.transpose(
-                        h_t[:, u, :], h_pairs[:, first : (n + 1) * 2 * P : 2], ident_f32[:]
-                    )
-                h_banks[(i, n)] = h_t
+            h_words[i] = norm_pool.tile(
+                [P, H_PASSES, P, PACK], BF16, name="h_words", align_bytes=64
+            )
+            h_banks[i] = []
+            for passes in H_BANKS:
+                h_t = psum.tile([P, len(passes), 2, P], F32, tag="bank", name="h_t")
+                for slot in range(len(passes)):
+                    for u in range(2):
+                        first = passes[slot] * 2 * P + u
+                        nc.tensor.transpose(
+                            h_t[:, slot, u, :],
+                            h_pairs[:, first : first - u + 2 * P : 2],
+                            ident_f32[:],
+                        )
+                h_banks[i].append(h_t)
 
         def copy_h(i):
-            for n in range(H_PASSES):
-                words = norm_pool.tile([P, P, PACK], BF16, bufs=6, align_bytes=64)
+            words = h_words[i][:].rearrange("p g r t -> p (g r t)").bitcast(F32)
+            words = words.rearrange("p (g r u) -> p g r u", g=H_PASSES, u=2)
+            for passes, h_t in zip(H_BANKS, h_banks[i]):
                 nc.scalar.copy(
-                    out=words[:].rearrange("p r t -> p (r t)").bitcast(F32).rearrange(
-                        "p (r u) -> p r u", u=2
-                    ),
-                    in_=h_banks[(i, n)][:].rearrange("p u r -> p r u"),
+                    out=words[:, passes[0] : passes[-1] + 1],
+                    in_=h_t[:].rearrange("p g u r -> p g r u"),
                 )
-                h_words[(i, n)] = words
 
         def quantise_h(i):
-            for n in range(H_PASSES):
-                quantise(h_words[(i, n)][:], h_codes[:, i, n, :], h_scales[:, i, n, :])
+            for passes in H_BANKS:
+                some = slice(passes[0], passes[-1] + 1)
+                nc.vector.quantize_mx(
+                    out=h_codes[:, i, some, :].rearrange("p g r -> p (g r)").bitcast(FP8X4),
+                    scales=h_scales[:, i, some, :].rearrange("p g r -> p (g r)"),
+                    in_=h_words[i][:, some].rearrange("p g r t -> p (g r t)"),
+                )
 
         def multiply_again(i):
             c_banks[i] = new_c_banks(i)

@@ -276,7 +276,7 @@ def tile_multiheadlatentattention_pa_kernel(tc, x, Wqa, q_a_norm_w, Wqb, out):
         cos_table, sin_table = build_rope_tables(nc, const)
 
         wqb_pool = ctx.enter_context(tc.tile_pool(name="wqb_raw", bufs=7, reuse_waits="tile"))
-        rope_pool = ctx.enter_context(tc.tile_pool(name="rope", bufs=4, reuse_waits="tile"))
+        rope_pool = ctx.enter_context(tc.tile_pool(name="rope", bufs=3, reuse_waits="tile"))
 
         wqb_tiles = {}
 
@@ -435,7 +435,7 @@ def tile_multiheadlatentattention_pa_kernel(tc, x, Wqa, q_a_norm_w, Wqb, out):
                     )
 
         def copy_nope(r, i):
-            results[(r, i)] = rope_pool.tile([P, GROUP_HEADS, D_HEAD], F32, name="result", bufs=6)
+            results[(r, i)] = rope_pool.tile([P, GROUP_HEADS, D_HEAD], F32, name="result", bufs=8)
             nc.scalar.copy(
                 out=results[(r, i)][:, :, 0:D_NOPE],
                 in_=nope_q[(r, i)][:].rearrange("p (h f) -> p h f", f=D_NOPE),

from contextlib import ExitStack
import math

import concourse.mybir as mybir
from concourse.masks import make_identity

F32 = mybir.dt.float32
BF16 = mybir.dt.bfloat16
I32 = mybir.dt.int32
U32 = mybir.dt.uint32
U8 = mybir.dt.uint8
FP8X4 = mybir.dt.float8_e4m3fn_x4
ALU = mybir.AluOpType
ACT = mybir.ActivationFunctionType

P = 128
PACK = 4
K_PASS = P * PACK
BANK = 512

BATCH, SEQ, D_MODEL, HEADS, D_NOPE, D_ROPE, RANK = 2, 256, 2048, 16, 64, 128, 1536
D_HEAD = D_NOPE + D_ROPE
THETA = 10000.0
EPS = 1e-6
N_FREQ = D_ROPE // 2

TOK_TILES = BATCH * SEQ // P
SEQ_TILES = SEQ // P
X_PASSES = D_MODEL // K_PASS
H_PASSES = RANK // K_PASS
RANK_BANKS = RANK // BANK
GROUP_HEADS = 4
GROUPS = HEADS // GROUP_HEADS
GROUP_COLS = GROUP_HEADS * D_HEAD
ROPE_COLS = GROUP_HEADS * D_ROPE
NOPE_COLS = GROUP_HEADS * D_NOPE
ROUND_MAGIC = 12582912.0

RUN = 8

BLOCKS = X_PASSES * RANK_BANKS

FLOPS = 2 * BATCH * SEQ * (D_MODEL * RANK + RANK * HEADS * D_HEAD)


def regroup(copy, grouped, rows):
    copy(
        out=grouped.rearrange("p (n c i) t -> p n c t i", n=rows.shape[2], i=RUN),
        in_=rows.rearrange("p t n (c i) -> p n c t i", i=RUN),
    )


def build_rope_tables(nc, const):
    position_int = const.tile([P, SEQ_TILES], I32)
    nc.gpsimd.iota(position_int[:], pattern=[[P, SEQ_TILES]], base=0, channel_multiplier=1)
    position = const.tile([P, SEQ_TILES], F32)
    nc.vector.tensor_copy(out=position[:], in_=position_int[:])

    freq = const.tile([P, N_FREQ], F32)
    nc.vector.memset(freq[:, 0:1], 1.0)
    for level in range(6):
        span = 1 << level
        nc.vector.tensor_scalar(
            out=freq[:, span : 2 * span],
            in0=freq[:, 0:span],
            scalar1=THETA ** (-span / N_FREQ),
            scalar2=None,
            op0=ALU.mult,
        )

    turns = const.tile([P, 2, SEQ_TILES, N_FREQ], F32)
    for a in range(SEQ_TILES):
        nc.vector.tensor_scalar(
            out=turns[:, 0, a, :],
            in0=freq[:],
            scalar1=position[:, a : a + 1],
            scalar2=1.0 / (2.0 * math.pi),
            op0=ALU.mult,
            op1=ALU.mult,
        )
    nc.vector.tensor_scalar(
        out=turns[:, 1], in0=turns[:, 0], scalar1=0.25, scalar2=None, op0=ALU.add
    )
    whole = const.tile([P, 2, SEQ_TILES, N_FREQ], F32)
    nc.vector.tensor_scalar(
        out=whole[:],
        in0=turns[:],
        scalar1=ROUND_MAGIC,
        scalar2=ROUND_MAGIC,
        op0=ALU.add,
        op1=ALU.subtract,
    )
    part = const.tile([P, 2, SEQ_TILES, N_FREQ], F32)
    nc.vector.tensor_tensor(out=part[:], in0=turns[:], in1=whole[:], op=ALU.subtract)
    trig = const.tile([P, 2, SEQ_TILES, N_FREQ], F32)
    nc.scalar.activation(out=trig[:], in_=part[:], func=ACT.Sin, scale=2.0 * math.pi)
    sin_pairs = trig[:, 0].rearrange("p a (i e) -> p a i e", e=2)
    nc.gpsimd.tensor_scalar(
        out=sin_pairs[:, :, :, 0],
        in0=sin_pairs[:, :, :, 0],
        scalar1=-1.0,
        scalar2=None,
        op0=ALU.mult,
    )
    return trig[:, 1], trig[:, 0]


def tile_multiheadlatentattention_pa_kernel(tc, x, Wqa, q_a_norm_w, Wqb, out):
    nc = tc.nc
    x_rows = x.flatten_outer_dims()

    with ExitStack() as ctx:
        const = ctx.enter_context(tc.tile_pool(name="const", bufs=1))
        keep = ctx.enter_context(tc.tile_pool(name="keep", bufs=1))
        late_x_pool = ctx.enter_context(tc.tile_pool(name="late_x", bufs=2))
        grouped_pool = ctx.enter_context(tc.tile_pool(name="grouped", bufs=4))
        norm_pool = ctx.enter_context(tc.tile_pool(name="norm", bufs=2))
        psum = ctx.enter_context(tc.psum_pool(name="psum", bufs=8))

        x_codes = keep.tile([P, TOK_TILES, X_PASSES * P], U32, align_bytes=64)
        x_scales = keep.tile([P, TOK_TILES, X_PASSES * P], U8, align_bytes=64)
        wqa_codes = keep.tile([P, X_PASSES, RANK], U32, align_bytes=64)
        wqa_scales = keep.tile([P, X_PASSES, RANK], U8, align_bytes=64)
        h_codes = keep.tile([P, TOK_TILES, H_PASSES, P], U32, align_bytes=64)
        h_scales = keep.tile([P, TOK_TILES, H_PASSES, P], U8, align_bytes=64)
        rope_codes = keep.tile([P, GROUPS, H_PASSES, ROPE_COLS], U32, align_bytes=64)
        rope_scales = keep.tile([P, GROUPS, H_PASSES, ROPE_COLS], U8, align_bytes=64)
        nope_codes = keep.tile([P, GROUPS, H_PASSES, NOPE_COLS], U32, align_bytes=64)
        nope_scales = keep.tile([P, GROUPS, H_PASSES, NOPE_COLS], U8, align_bytes=64)

        ident_f32 = const.tile([P, P], F32)
        make_identity(nc, ident_f32[:])
        gain_row = const.tile([P, RANK], BF16)
        nc.gpsimd.memset(gain_row[:].bitcast(I32), 0)
        ones = const.tile([P, P], BF16)
        gain = const.tile([P, RANK], BF16)
        minus_half = const.tile([P, 1], F32)

        def spread_gain():
            for n in range(RANK_BANKS):
                cols = slice(n * BANK, (n + 1) * BANK)
                gain_bank = psum.tile([P, BANK], BF16, tag="bank")
                nc.tensor.matmul(
                    out=gain_bank[:], lhsT=ones[:], rhs=gain_row[:, cols], start=True, stop=True
                )
                nc.scalar.copy(out=gain[:, cols], in_=gain_bank[:])

        def quantise(grouped, codes, scales):
            nc.vector.quantize_mx(
                out=codes.bitcast(FP8X4), scales=scales, in_=grouped.rearrange("p c t -> p (c t)")
            )

        def new_c_banks(i):
            return [
                psum.tile([P, BANK], F32, tag="bank", name="c_%d_%d" % (i, n))
                for n in range(RANK_BANKS)
            ]

        c_banks = {}

        def first_matmul(i, g, n):
            nc.tensor.matmul_mx(
                out=c_banks[i][n][:],
                lhsT=x_codes[:, i, g * P : (g + 1) * P].bitcast(FP8X4),
                lhsT_scale=x_scales[:, i, g * P : (g + 1) * P],
                rhs=wqa_codes[:, g, n * BANK : (n + 1) * BANK].bitcast(FP8X4),
                rhs_scale=wqa_scales[:, g, n * BANK : (n + 1) * BANK],
                start=(g == 0),
                stop=(g == X_PASSES - 1),
            )

        x_tiles = {}
        x_grouped = {}

        def load_x(i, pool):
            x_sb = pool.tile([P, D_MODEL], BF16, name="x_sb")
            nc.sync.dma_start(out=x_sb[:], in_=x_rows[i * P : (i + 1) * P, :])
            x_tiles[i] = x_sb

        def transpose_x(i):
            x_words = x_tiles[i][:].bitcast(F32)
            x_grouped[i] = late_x_pool.tile([P, D_MODEL], BF16, name="x_grouped", align_bytes=64)
            x_grouped_words = x_grouped[i][:].bitcast(F32).rearrange(
                "p (g r u) -> p g r u", g=X_PASSES, u=2
            )
            for half in range(2):
                x_t = psum.tile([P, 2, 2, P], F32, tag="bank")
                for gg in range(2):
                    for u in range(2):
                        first = (2 * half + gg) * 2 * P
                        nc.tensor.transpose(
                            x_t[:, gg, u, :],
                            x_words[:, first + u : first + 2 * P : 2],
                            ident_f32[:],
                        )
                nc.scalar.copy(
                    out=x_grouped_words[:, 2 * half : 2 * half + 2],
                    in_=x_t[:].rearrange("p g u r -> p g r u"),
                )

        def quantise_x(i):
            nc.vector.quantize_mx(
                out=x_codes[:, i, :].bitcast(FP8X4), scales=x_scales[:, i, :], in_=x_grouped[i][:]
            )

        with tc.tile_pool(name="x", bufs=2) as x_pool, tc.tile_pool(name="wqa_raw", bufs=1) as wqa_pool:
            wqa_blocks = {}

            def load_wqa(g, first, blocks):
                wqa_raw = wqa_pool.tile(
                    [P, PACK, blocks * BANK], BF16, name="wqa_raw_%d_%d" % (g, first)
                )
                nc.sync.dma_start(
                    out=wqa_raw[:],
                    in_=Wqa[
                        g * K_PASS : (g + 1) * K_PASS, first * BANK : (first + blocks) * BANK
                    ].rearrange("(p t) c -> p t c", t=PACK),
                )
                for n in range(blocks):
                    wqa_blocks[(g, first + n)] = wqa_raw[:, :, n * BANK : (n + 1) * BANK]

            load_wqa(0,0,1)
            load_wqa(0,1,1)
            load_wqa(0,2,1)
            load_wqa(1,0,1)
            load_wqa(1,1,2)
            load_x(0, x_pool)
            load_x(1, x_pool)
            nc.sync.dma_start(out=gain_row[0:1, :], in_=q_a_norm_w.unsqueeze(0))
            load_wqa(2,0,3)
            load_wqa(3,0,1)
            load_wqa(3,1,2)

            nc.gpsimd.memset(ones[:], 1.0)
            nc.gpsimd.memset(minus_half[:], -0.5)

            grouped = {}

            def regroup_wqa(b):
                g, n = divmod(b, RANK_BANKS)
                grouped[b] = grouped_pool.tile(
                    [P, BANK, PACK], BF16, name="wqa_grouped", tag="grouped_512", align_bytes=64
                )
                regroup(
                    nc.vector.tensor_copy if b % 2 == 0 or b == BLOCKS - 1 else nc.scalar.copy,
                    grouped[b][:],
                    wqa_blocks[(g, n)].unsqueeze(2),
                )

            def quantise_wqa(b):
                g, n = divmod(b, RANK_BANKS)
                cols = slice(n * BANK, (n + 1) * BANK)
                quantise(grouped[b][:], wqa_codes[:, g, cols], wqa_scales[:, g, cols])

            for i in range(2):
                c_banks[i] = new_c_banks(i)
            for b in range(BLOCKS + 2):
                if b < BLOCKS:
                    regroup_wqa(b)
                if b in (5, 6):
                    transpose_x(b - 5)
                if b in (7, 8):
                    quantise_x(b - 7)
                if b >= 2:
                    quantise_wqa(b - 2)
                if b >= 9:
                    g = b - 9
                    if g < X_PASSES - 1:
                        for i in range(2):
                            for n in range(RANK_BANKS):
                                first_matmul(i, g, n)
            for i in range(2):
                for n in range(RANK_BANKS):
                    first_matmul(i, X_PASSES - 1, n)

        cos_table, sin_table = build_rope_tables(nc, const)

        wqb_pool = ctx.enter_context(tc.tile_pool(name="wqb_raw", bufs=7, reuse_waits="tile"))
        rope_pool = ctx.enter_context(tc.tile_pool(name="rope", bufs=3, reuse_waits="tile"))

        wqb_tiles = {}

        def load_wqb(unit):
            r, g = divmod(unit, H_PASSES)
            wqb_raw = wqb_pool.tile([P, PACK, GROUP_COLS], BF16, name="wqb_raw")
            nc.sync.dma_start(
                out=wqb_raw[:],
                in_=Wqb[
                    g * K_PASS : (g + 1) * K_PASS, r * GROUP_COLS : (r + 1) * GROUP_COLS
                ].rearrange("(p t) c -> p t c", t=PACK),
            )
            wqb_tiles[unit] = wqb_raw[:].rearrange("p t (h f) -> p t h f", f=D_HEAD)

        for unit in range(7):
            load_wqb(unit)
            if unit < 2:
                load_x(unit + 2, late_x_pool)

        rope_grouped = {}
        nope_grouped = {}

        def regroup_rope(unit, copy, halves=(0, 1)):
            if 0 in halves:
                rope_grouped[unit] = grouped_pool.tile(
                    [P, ROPE_COLS, PACK], BF16, name="rope_grouped", tag="grouped_512", align_bytes=64
                )
            for half in halves:
                regroup(
                    copy,
                    rope_grouped[unit][:, half * 2 * D_ROPE : (half + 1) * 2 * D_ROPE, :],
                    wqb_tiles[unit][:, :, 2 * half : 2 * half + 2, D_NOPE:D_HEAD],
                )

        def regroup_nope(unit, copy):
            nope_grouped[unit] = grouped_pool.tile(
                [P, NOPE_COLS, PACK], BF16, name="nope_grouped", tag="grouped_256", align_bytes=64
            )
            regroup(copy, nope_grouped[unit][:], wqb_tiles[unit][:, :, :, 0:D_NOPE])

        def quantise_rope(unit):
            r, g = divmod(unit, H_PASSES)
            quantise(rope_grouped[unit][:], rope_codes[:, r, g, :], rope_scales[:, r, g, :])

        def quantise_nope(unit):
            r, g = divmod(unit, H_PASSES)
            quantise(nope_grouped[unit][:], nope_codes[:, r, g, :], nope_scales[:, r, g, :])

        sum_sq = {}
        rstd = {}
        h_rows = {}
        h_banks = {}
        h_words = {}
        H_BANKS = ((0, 1), (2,))

        def square(i):
            sum_sq[i] = norm_pool.tile([P, RANK_BANKS], F32, name="sum_sq")
            for n in range(RANK_BANKS):
                squares = norm_pool.tile([P, BANK], BF16)
                nc.scalar.activation(
                    out=squares[:],
                    in_=c_banks[i][n][:],
                    func=ACT.Square,
                    accum_out=sum_sq[i][:, n : n + 1],
                )

        def inverse_rms(i):
            rstd[i] = norm_pool.tile([P, 1], F32, name="rstd")
            shares = norm_pool.tile([P, RANK_BANKS], F32)
            nc.vector.tensor_scalar(
                out=shares[:],
                in0=sum_sq[i][:],
                scalar1=1.0 / RANK,
                scalar2=EPS,
                op0=ALU.mult,
                op1=ALU.add,
                accum_out=rstd[i][:],
            )
            nc.gpsimd.tensor_tensor(out=rstd[i][:], in0=rstd[i][:], in1=minus_half[:], op=ALU.pow)

        def scale_h(i):
            h_rows[i] = norm_pool.tile([P, RANK], BF16, name="h_rows")
            for n in range(RANK_BANKS):
                cols = slice(n * BANK, (n + 1) * BANK)
                nc.vector.scalar_tensor_tensor(
                    out=h_rows[i][:, cols],
                    in0=c_banks[i][n][:],
                    scalar=rstd[i][:, 0:1],
                    in1=gain[:, cols],
                    op0=ALU.mult,
                    op1=ALU.mult,
                )

        def transpose_h(i):
            h_pairs = h_rows[i][:].bitcast(F32)
            h_words[i] = norm_pool.tile(
                [P, H_PASSES, P, PACK], BF16, name="h_words", align_bytes=64
            )
            h_banks[i] = []
            for passes in H_BANKS:
                h_t = psum.tile([P, len(passes), 2, P], F32, tag="bank", name="h_t")
                for slot in range(len(passes)):
                    for u in range(2):
                        first = passes[slot] * 2 * P + u
                        nc.tensor.transpose(
                            h_t[:, slot, u, :],
                            h_pairs[:, first : first - u + 2 * P : 2],
                            ident_f32[:],
                        )
                h_banks[i].append(h_t)

        def copy_h(i):
            words = h_words[i][:].rearrange("p g r t -> p (g r t)").bitcast(F32)
            words = words.rearrange("p (g r u) -> p g r u", g=H_PASSES, u=2)
            for passes, h_t in zip(H_BANKS, h_banks[i]):
                nc.scalar.copy(
                    out=words[:, passes[0] : passes[-1] + 1],
                    in_=h_t[:].rearrange("p g u r -> p g r u"),
                )

        def quantise_h(i):
            for passes in H_BANKS:
                some = slice(passes[0], passes[-1] + 1)
                nc.vector.quantize_mx(
                    out=h_codes[:, i, some, :].rearrange("p g r -> p (g r)").bitcast(FP8X4),
                    scales=h_scales[:, i, some, :].rearrange("p g r -> p (g r)"),
                    in_=h_words[i][:, some].rearrange("p g r t -> p (g r t)"),
                )

        def multiply_again(i):
            c_banks[i] = new_c_banks(i)
            for n in range(RANK_BANKS):
                for g in range(X_PASSES):
                    first_matmul(i, g, n)

        rope_q = {}
        nope_q = {}
        results = {}

        def second_matmul(r, i):
            rope_q[(r, i)] = psum.tile([P, ROPE_COLS], F32, tag="bank", name="rope_q")
            nope_q[(r, i)] = psum.tile([P, NOPE_COLS], F32, tag="bank", name="nope_q")
            for q_bank, codes, scales in (
                (rope_q[(r, i)], rope_codes, rope_scales),
                (nope_q[(r, i)], nope_codes, nope_scales),
            ):
                for g in range(H_PASSES):
                    nc.tensor.matmul_mx(
                        out=q_bank[:],
                        lhsT=h_codes[:, i, g, :].bitcast(FP8X4),
                        lhsT_scale=h_scales[:, i, g, :],
                        rhs=codes[:, r, g, :].bitcast(FP8X4),
                        rhs_scale=scales[:, r, g, :],
                        start=(g == 0),
                        stop=(g == H_PASSES - 1),
                    )

        def copy_nope(r, i):
            results[(r, i)] = rope_pool.tile([P, GROUP_HEADS, D_HEAD], F32, name="result", bufs=8)
            nc.scalar.copy(
                out=results[(r, i)][:, :, 0:D_NOPE],
                in_=nope_q[(r, i)][:].rearrange("p (h f) -> p h f", f=D_NOPE),
            )

        repeats = ROPE_COLS // N_FREQ

        def rotate(r, i, adder):
            a = i % SEQ_TILES
            bank = rope_q[(r, i)]
            straight = rope_pool.tile([P, ROPE_COLS], F32)
            nc.vector.tensor_tensor(
                out=straight[:].rearrange("p (m j) -> p m j", j=N_FREQ),
                in0=bank[:].rearrange("p (m j) -> p m j", j=N_FREQ),
                in1=cos_table[:, a, :].unsqueeze(1).to_broadcast([P, repeats, N_FREQ]),
                op=ALU.mult,
            )
            crossed = rope_pool.tile([P, ROPE_COLS], F32)
            nc.vector.tensor_tensor(
                out=crossed[:].rearrange("p (m i e) -> p m i e", i=N_FREQ // 2, e=2),
                in0=bank[:].rearrange("p (m i e) -> p m i e", i=N_FREQ // 2, e=2)[:, :, :, ::-1],
                in1=sin_table[:, a, :]
                .rearrange("p (i e) -> p i e", e=2)
                .unsqueeze(1)
                .to_broadcast([P, repeats, N_FREQ // 2, 2]),
                op=ALU.mult,
            )
            adder.tensor_tensor(
                out=results[(r, i)][:, :, D_NOPE:D_HEAD],
                in0=straight[:].rearrange("p (h f) -> p h f", h=GROUP_HEADS),
                in1=crossed[:].rearrange("p (h f) -> p h f", h=GROUP_HEADS),
                op=ALU.add,
            )
            nc.sync.dma_start(
                out=out[
                    i // SEQ_TILES, r * GROUP_HEADS : (r + 1) * GROUP_HEADS, a * P : (a + 1) * P, :
                ].rearrange("h s f -> s h f"),
                in_=results[(r, i)][:],
            )

        vector_copy = nc.vector.tensor_copy
        scalar_copy = nc.scalar.copy

        transpose_x(2)
        quantise_x(2)
        spread_gain()
        square(0)
        regroup_nope(0, vector_copy)
        transpose_x(3)
        square(1)
        inverse_rms(0)
        quantise_x(3)
        scale_h(0)
        transpose_h(0)
        regroup_rope(0, scalar_copy)
        quantise_nope(0)
        inverse_rms(1)
        multiply_again(2)
        scale_h(1)
        transpose_h(1)
        copy_h(0)
        regroup_nope(1, vector_copy)
        regroup_rope(1, scalar_copy)
        quantise_h(0)
        quantise_rope(0)
        copy_h(1)
        square(2)
        multiply_again(3)
        regroup_nope(2, vector_copy)
        quantise_nope(1)
        quantise_h(1)
        inverse_rms(2)
        quantise_rope(1)
        regroup_rope(2, vector_copy)
        scale_h(2)
        transpose_h(2)
        square(3)
        quantise_nope(2)
        quantise_rope(2)
        copy_h(2)
        inverse_rms(3)
        second_matmul(0, 0)
        quantise_h(2)
        scale_h(3)
        transpose_h(3)
        regroup_rope(3, scalar_copy)
        regroup_nope(3, vector_copy)
        copy_h(3)
        second_matmul(0, 1)
        quantise_h(3)
        quantise_rope(3)
        quantise_nope(3)
        for unit in range(7, H_PASSES * GROUPS):
            load_wqb(unit)

        steps = [(r, i) for r in range(GROUPS) for i in range(TOK_TILES)]
        for s in range(len(steps)):
            r, i = steps[s]
            unit = H_PASSES * r + 4 + i
            if i < H_PASSES and unit < H_PASSES * GROUPS:
                regroup_rope(unit, scalar_copy)
                regroup_nope(unit, vector_copy if unit < 9 else scalar_copy)
            copy_nope(r, i)
            rotate(r, i, nc.vector if s >= len(steps) - 2 else nc.gpsimd)
            if i > 0 and unit - 1 < H_PASSES * GROUPS:
                quantise_rope(unit - 1)
                quantise_nope(unit - 1)
            if s + 2 < len(steps):
                second_matmul(*steps[s + 2])
